import numpy as np
import ml_dtypes


def mxq(x, axis, fmt="e4m3"):
    dtype, down = {"e4m3": (ml_dtypes.float8_e4m3fn, 7), "e5m2": (ml_dtypes.float8_e5m2, 14)}[fmt]
    v = np.moveaxis(np.asarray(x, np.float32).astype(ml_dtypes.bfloat16).astype(np.float64), axis, -1)
    blocks = v.reshape(v.shape[:-1] + (-1, 32))
    amax = np.abs(blocks).max(-1, keepdims=True)
    byte = np.maximum(np.where(amax > 0, np.frexp(amax)[1] - 1 + 127, 0) - down, 1)
    scale = np.exp2(byte - 127.0)
    codes = (blocks / scale).astype(np.float32).astype(dtype).astype(np.float64)
    return np.moveaxis((codes * scale).reshape(v.shape), -1, axis)


WIDE = False


def mx_kscale(k):
    if not WIDE:
        return np.ones(k)
    levels = np.array([10, -10, 5, -5, 0])
    a = np.random.permutation(np.resize(levels, k // 512 * 4)).reshape(k // 512, 4)
    idx = np.arange(k)
    return np.exp2(a[idx // 512, idx % 128 // 32])


BF16 = ml_dtypes.bfloat16


def bf(x):
    return np.asarray(x, np.float32).astype(BF16)


def f64(x):
    return np.asarray(x).astype(np.float64)


B, L, DIM, H, D = 4, 2048, 1024, 2, 64
EPS = 1e-6
THETA = 10000.0


def rope_table(seq_len, head_dim):
    pos = np.arange(seq_len, dtype=np.float64)
    inv = 1.0 / (THETA ** (np.arange(0, head_dim, 2, dtype=np.float64) / head_dim))
    ang = pos[:, None] * inv[None, :]
    cos, sin = np.cos(ang), np.sin(ang)
    rot = np.stack([np.stack([cos, -sin], -1), np.stack([sin, cos], -1)], -2)
    return rot[None, None]


def rms_norm(u, gain):
    rrms = 1.0 / np.sqrt(np.mean(np.square(u), axis=-1, keepdims=True) + EPS)
    return u * rrms * gain


def rope(u, table):
    ur = u.reshape(*u.shape[:-1], -1, 1, 2)
    out = table[..., 0] * ur[..., 0] + table[..., 1] * ur[..., 1]
    return out.reshape(u.shape)


def setup_inputs():
    s = mx_kscale(DIM)
    return {"x": bf(np.random.standard_normal((B, L, DIM)) * s),
            "pe": bf(rope_table(L, D)),
            "qkv_w": bf(np.random.standard_normal((DIM, 3 * H * D)) / np.sqrt(DIM) / s[:, None]),
            "qkv_b": bf(np.random.standard_normal(3 * H * D) * 0.2),
            "q_scale": bf(1.0 + 0.1 * np.random.standard_normal(D)),
            "k_scale": bf(1.0 + 0.1 * np.random.standard_normal(D))}


def reference(x, pe, qkv_w, qkv_b, q_scale, k_scale):
    qkv = (mxq(f64(x), 2, "e4m3") @ mxq(f64(qkv_w), 0, "e4m3")) + f64(qkv_b)
    qkv = qkv.reshape(B, L, 3, H, D).transpose(2, 0, 3, 1, 4)
    q, k, v = qkv[0], qkv[1], qkv[2]
    q = rms_norm(q, f64(q_scale))
    k = rms_norm(k, f64(k_scale))
    table = f64(pe)
    return rope(q, table), rope(k, table), v

@@ -1,0 +1,266 @@
+from contextlib import ExitStack
+
+import concourse.mybir as mybir
+from concourse.masks import make_identity
+
+F32 = mybir.dt.float32
+BF16 = mybir.dt.bfloat16
+U32 = mybir.dt.uint32
+U8 = mybir.dt.uint8
+FP8X4 = mybir.dt.float8_e4m3fn_x4
+ALU = mybir.AluOpType
+ACT = mybir.ActivationFunctionType
+
+B, L, DIM, H, D = 4, 2048, 1024, 2, 64
+EPS = 1e-6
+P = 128
+TPB = L // P
+RT = 4
+ROUNDS = B * TPB // RT
+NX = 6
+FLOPS = 2 * B * L * DIM * 3 * H * D
+PIN = True
+
+
+def tile_selfattention_pa_t_kernel(tc, x, pe, qkv_w, qkv_b, q_scale, k_scale, out_0, out_1, out_2):
+    nc = tc.nc
+    with ExitStack() as ctx:
+        const = ctx.enter_context(tc.tile_pool(name="const", bufs=1))
+        xpool = ctx.enter_context(tc.tile_pool(name="xpool", bufs=NX))
+        gpool = ctx.enter_context(tc.tile_pool(name="gpool", bufs=2))
+        cpool = ctx.enter_context(tc.tile_pool(name="cpool", bufs=2))
+        ypool = ctx.enter_context(tc.tile_pool(name="ypool", bufs=2))
+        ppool = ctx.enter_context(tc.tile_pool(name="ppool", bufs=2))
+        spool = ctx.enter_context(tc.tile_pool(name="spool", bufs=2))
+        small = ctx.enter_context(tc.tile_pool(name="small", bufs=3))
+        stage = ctx.enter_context(tc.tile_pool(name="stage", bufs=2))
+        psum_tp = ctx.enter_context(tc.psum_pool(name="psum_tp", bufs=4))
+        psum_qk = ctx.enter_context(tc.psum_pool(name="psum_qk", bufs=2))
+        psum_v = ctx.enter_context(tc.psum_pool(name="psum_v", bufs=2))
+        if PIN:
+            ctx.enter_context(tc.manual_schedule())
+
+        xts, tps, groupeds, codes, planes = {}, {}, {}, {}, {}
+        qkbanks, vbanks, ys, prods, sums, rrs, stages = {}, {}, {}, {}, {}, {}, {}
+
+        def load(r):
+            b, j = divmod(r, TPB // RT)
+            xt = xpool.tile([P, RT * DIM], BF16, name="xt", tag="xt")
+            src = x[b].rearrange("(p t) k -> p (t k)", t=TPB)
+            nc.sync.dma_start(out=xt[:], in_=src[:, j * RT * DIM:(j + 1) * RT * DIM])
+            xts[r] = xt
+
+        ident = const.tile([P, P], F32, name="ident", tag="ident")
+        make_identity(nc, ident[:])
+        ones = const.tile([P, P], BF16, name="ones", tag="ones")
+        nc.vector.memset(ones[:], 1.0)
+        row = const.tile([P, 512], BF16, name="row", tag="row")
+        nc.vector.memset(row[:], 0.0)
+        eps = const.tile([P, 1], F32, name="eps", tag="eps")
+        nc.vector.memset(eps[:], EPS)
+        junk = const.tile([P, D], F32, name="junk", tag="junk")
+
+        w_raw = const.tile([P, 8, 384], BF16, name="w_raw", tag="w_raw")
+        nc.sync.dma_start(
+            out=w_raw[:].rearrange("p (c e) n -> p c (e n)", e=2),
+            in_=qkv_w.rearrange("(c q e) n -> q c (e n)", c=4, e=2),
+        )
+        nc.sync.dma_start(out=row[0:1, 0:384], in_=qkv_b.unsqueeze(0))
+        nc.sync.dma_start(out=row[0:1, 384:448], in_=q_scale.unsqueeze(0))
+        nc.sync.dma_start(out=row[0:1, 448:512], in_=k_scale.unsqueeze(0))
+        load(0)
+        pe_sb = const.tile([P, TPB * 128], BF16, name="pe_sb", tag="pe_sb")
+        nc.sync.dma_start(out=pe_sb[:], in_=pe[0, 0].rearrange("(p t) i a b -> p (t i a b)", t=TPB))
+        for r in range(1, NX):
+            load(r)
+        nc.scalar.activation(out=junk[:, 0:1], in_=eps[:], func=ACT.Abs_reciprocal_sqrt)
+
+        wg_qk = const.tile([P, 2, 256, 4], BF16, name="wg_qk", tag="wg_qk", align_bytes=64)
+        wg_v = const.tile([P, 2, 128, 4], BF16, name="wg_v", tag="wg_v", align_bytes=64)
+        for g in range(2):
+            for b in range(2):
+                nc.vector.tensor_copy(
+                    out=wg_qk[:, g].rearrange("p (n b i) t -> p n b i t", n=4, b=2)[:, :, b],
+                    in_=w_raw[:, 4 * g:4 * g + 4, 0:256].rearrange("p t (n i b) -> p n i t b", i=32, b=2)[:, :, :, :, b],
+                )
+            nc.vector.tensor_copy(out=wg_v[:, g], in_=w_raw[:, 4 * g:4 * g + 4, 256:384].rearrange("p t n -> p n t"))
+        wc_qk = const.tile([P, 512], U32, name="wc_qk", tag="wc_qk", align_bytes=64)
+        ws_qk = const.tile([P, 512], U8, name="ws_qk", tag="ws_qk", align_bytes=64)
+        wc_v = const.tile([P, 256], U32, name="wc_v", tag="wc_v", align_bytes=64)
+        ws_v = const.tile([P, 256], U8, name="ws_v", tag="ws_v", align_bytes=64)
+        nc.vector.quantize_mx(out=wc_qk[:].bitcast(FP8X4), scales=ws_qk[:], in_=wg_qk[:].rearrange("p g n t -> p (g n t)"))
+        nc.vector.quantize_mx(out=wc_v[:].bitcast(FP8X4), scales=ws_v[:], in_=wg_v[:].rearrange("p g n t -> p (g n t)"))
+
+        cps = psum_v.tile([P, 512], F32, name="cps", tag="vb")
+        nc.tensor.matmul(out=cps[:], lhsT=ones[:], rhs=row[:], start=True, stop=True)
+        bias_qk = const.tile([P, 256], F32, name="bias_qk", tag="bias_qk")
+        nc.vector.tensor_copy(
+            out=bias_qk[:].rearrange("p (n b i) -> p n b i", b=2, i=32),
+            in_=cps[:, 0:256].rearrange("p (n i b) -> p n b i", i=32, b=2),
+        )
+        cv = const.tile([P, 256], F32, name="cv", tag="cv")
+        nc.vector.tensor_copy(out=cv[:], in_=cps[:, 256:512])
+
+        tab = const.tile([P, TPB, 2, 2, D], F32, name="tab", tag="tab")
+        for s in range(2):
+            eng = nc.vector if s == 0 else nc.gpsimd
+            for b in range(2):
+                gain = cv[:, 128 + s * D:128 + (s + 1) * D].rearrange("p (i b) -> p b i", b=2)[:, b, :]
+                eng.tensor_tensor(
+                    out=tab[:, :, s, b, :].rearrange("p t (a i) -> p t a i", a=2),
+                    in0=pe_sb[:].rearrange("p (t i a b) -> p t a i b", i=32, a=2, b=2)[:, :, :, :, b],
+                    in1=gain.unsqueeze(1).unsqueeze(1).to_broadcast([P, TPB, 2, 32]),
+                    op=ALU.mult,
+                )
+
+        def transposes(r):
+            words = xts[r][:].bitcast(F32)
+            banks = []
+            for tt in range(RT):
+                tp = psum_tp.tile([P, 4, P], F32, name="tp", tag="tp")
+                for c in range(4):
+                    col = tt * 512 + c * P
+                    nc.tensor.transpose(tp[:, c, :], words[:, col:col + P], ident[:])
+                banks.append(tp)
+            tps[r] = banks
+            if r + NX < ROUNDS:
+                load(r + NX)
+
+        def copy_out(r):
+            grouped = gpool.tile([P, RT * DIM], BF16, name="grouped", tag="grouped", align_bytes=64)
+            gw = grouped[:].bitcast(F32)
+            for tt in range(RT):
+                nc.scalar.copy(
+                    out=gw[:, tt * 512:(tt + 1) * 512].rearrange("p (g r u) -> p g r u", g=2, u=2),
+                    in_=tps[r][tt][:].rearrange("p (g u) r -> p g r u", u=2),
+                )
+            groupeds[r] = grouped
+
+        def quantise(r):
+            xc = cpool.tile([P, RT * 256], U32, name="xc", tag="xc", align_bytes=64)
+            xs = cpool.tile([P, RT * 256], U8, name="xs", tag="xs", align_bytes=64)
+            nc.vector.quantize_mx(out=xc[:].bitcast(FP8X4), scales=xs[:], in_=groupeds[r][:])
+            codes[r], planes[r] = xc, xs
+
+        def project(r):
+            xc, xs = codes[r], planes[r]
+            qk = []
+            for hf in range(2):
+                qkb = psum_qk.tile([P, 512], F32, name="qkb", tag="qkb")
+                qk.append(qkb)
+            vb = psum_v.tile([P, 512], F32, name="vb", tag="vb")
+            for tt in range(RT):
+                for g in range(2):
+                    sl = slice((tt * 2 + g) * P, (tt * 2 + g + 1) * P)
+                    nc.tensor.matmul_mx(
+                        out=qk[tt // 2][:, (tt % 2) * 256:(tt % 2 + 1) * 256],
+                        lhsT=xc[:, sl].bitcast(FP8X4), lhsT_scale=xs[:, sl],
+                        rhs=wc_qk[:, g * 256:(g + 1) * 256].bitcast(FP8X4), rhs_scale=ws_qk[:, g * 256:(g + 1) * 256],
+                        start=(g == 0), stop=(g == 1),
+                    )
+                    nc.tensor.matmul_mx(
+                        out=vb[:, tt * P:(tt + 1) * P],
+                        lhsT=xc[:, sl].bitcast(FP8X4), lhsT_scale=xs[:, sl],
+                        rhs=wc_v[:, g * P:(g + 1) * P].bitcast(FP8X4), rhs_scale=ws_v[:, g * P:(g + 1) * P],
+                        start=(g == 0), stop=(g == 1),
+                    )
+            qkbanks[r], vbanks[r] = qk, vb
+
+        def store(dst, st, r):
+            b, j = divmod(r, TPB // RT)
+            hb = j // 2
+            view = dst[b].rearrange("h (p t) d -> p h (t d)", t=TPB)
+            nc.sync.dma_start(out=view[:, :, hb * 512:(hb + 1) * 512], in_=st[:].rearrange("p h t d -> p h (t d)"))
+
+        def add_bias(r):
+            y = ypool.tile([P, RT, 256], F32, name="y", tag="y")
+            for hf in range(2):
+                nc.vector.tensor_tensor(
+                    out=y[:, 2 * hf:2 * hf + 2, :],
+                    in0=qkbanks[r][hf][:].rearrange("p (t c) -> p t c", t=2),
+                    in1=bias_qk[:].unsqueeze(1).to_broadcast([P, 2, 256]),
+                    op=ALU.add,
+                )
+            ys[r] = y
+            if r % 2 == 0:
+                vst = stage.tile([P, H, 2 * RT, D], F32, name="vst", tag="vst")
+                stages["v", r // 2] = vst
+            vst = stages["v", r // 2]
+            tl = (r % 2) * RT
+            nc.vector.tensor_tensor(
+                out=vst[:, :, tl:tl + RT, :].rearrange("p h t d -> p t h d"),
+                in0=vbanks[r][:].rearrange("p (t h d) -> p t h d", t=RT, h=H),
+                in1=cv[:, 0:128].rearrange("p (h d) -> p h d", h=H).unsqueeze(1).to_broadcast([P, RT, H, D]),
+                op=ALU.add,
+            )
+            if r % 2 == 1:
+                store(out_2, vst, r)
+
+        def squares(r):
+            ss = small.tile([P, 4 * RT], F32, name="ss", tag="ss")
+            for n in range(4 * RT):
+                nc.scalar.activation(
+                    out=junk[:], in_=ys[r][:, n // 4, (n % 4) * D:(n % 4 + 1) * D],
+                    func=ACT.Square, accum_out=ss[:, n:n + 1],
+                )
+            rr = small.tile([P, 4 * RT], F32, name="rr", tag="rr")
+            nc.scalar.activation(out=rr[:], in_=ss[:], func=ACT.Abs_reciprocal_sqrt, scale=1.0 / D, bias=eps[:])
+            rrs[r] = rr
+
+        def products(r):
+            t0 = (r % (TPB // RT)) * RT
+            pr = ppool.tile([P, 4 * RT, 2, D], F32, name="pr", tag="pr")
+            shape = [P, 2 * RT, H, 2, 2, 32]
+            nc.vector.tensor_tensor(
+                out=pr[:].rearrange("p (m h) b (a i) -> p m h b a i", h=H, a=2),
+                in0=ys[r][:].rearrange("p t (s h b i) -> p (t s) h b i", s=2, h=H, b=2).unsqueeze(4).to_broadcast(shape),
+                in1=tab[:, t0:t0 + RT].rearrange("p t s b (a i) -> p (t s) b a i", a=2).unsqueeze(2).to_broadcast(shape),
+                op=ALU.mult,
+            )
+            prods[r] = pr
+
+        def pair_add(r):
+            sm = spool.tile([P, 4 * RT, D], F32, name="sm", tag="sm")
+            nc.vector.tensor_tensor(out=sm[:], in0=prods[r][:, :, 0, :], in1=prods[r][:, :, 1, :], op=ALU.add)
+            sums[r] = sm
+
+        def scale_out(r):
+            if r % 2 == 0:
+                qst = stage.tile([P, H, 2 * RT, D], F32, name="qst", tag="qst")
+                kst = stage.tile([P, H, 2 * RT, D], F32, name="kst", tag="kst")
+                stages["q", r // 2], stages["k", r // 2] = qst, kst
+            sts = (stages["q", r // 2], stages["k", r // 2])
+            tl = (r % 2) * RT
+            for n in range(4 * RT):
+                tt, s, h = n // 4, (n // 2) % 2, n % 2
+                nc.scalar.activation(
+                    out=sts[s][:, h, tl + tt, :].rearrange("p (i a) -> p i a", a=2),
+                    in_=sums[r][:, n, :].rearrange("p (a i) -> p i a", a=2),
+                    func=ACT.Copy, scale=rrs[r][:, n:n + 1],
+                )
+            if r % 2 == 1:
+                store(out_0, sts[0], r)
+                store(out_1, sts[1], r)
+
+        def live(r):
+            return 0 <= r < ROUNDS
+
+        transposes(0)
+        for i in range(-2, ROUNDS + 1):
+            if live(i + 2):
+                copy_out(i + 2)
+            if live(i + 1):
+                quantise(i + 1)
+            if live(i):
+                add_bias(i)
+            if live(i + 1):
+                project(i + 1)
+            if live(i + 3):
+                transposes(i + 3)
+            if live(i):
+                squares(i)
+            if live(i - 1):
+                pair_add(i - 1)
+                scale_out(i - 1)
+            if live(i):
+                products(i)

@@ -32,6 +32,7 @@ def tile_selfattention_pa_t_kernel(tc, x, pe, qkv_w, qkv_b, q_scale, k_scale, ou
         ypool = ctx.enter_context(tc.tile_pool(name="ypool", bufs=2))
         ppool = ctx.enter_context(tc.tile_pool(name="ppool", bufs=2))
         spool = ctx.enter_context(tc.tile_pool(name="spool", bufs=2))
+        jpool = ctx.enter_context(tc.tile_pool(name="jpool", bufs=2))
         small = ctx.enter_context(tc.tile_pool(name="small", bufs=3))
         stage = ctx.enter_context(tc.tile_pool(name="stage", bufs=2))
         psum_tp = ctx.enter_context(tc.psum_pool(name="psum_tp", bufs=4))
@@ -198,9 +199,10 @@ def tile_selfattention_pa_t_kernel(tc, x, pe, qkv_w, qkv_b, q_scale, k_scale, ou
 
         def squares(r):
             ss = small.tile([P, 4 * RT], F32, name="ss", tag="ss")
+            sq = jpool.tile([P, 4 * RT, D], F32, name="sq", tag="sq")
             for n in range(4 * RT):
                 nc.scalar.activation(
-                    out=junk[:], in_=ys[r][:, n // 4, (n % 4) * D:(n % 4 + 1) * D],
+                    out=sq[:, n, :], in_=ys[r][:, n // 4, (n % 4) * D:(n % 4 + 1) * D],
                     func=ACT.Square, accum_out=ss[:, n:n + 1],
                 )
             rr = small.tile([P, 4 * RT], F32, name="rr", tag="rr")

@@ -20,6 +20,7 @@ ROUNDS = B * TPB // RT
 NX = 6
 FLOPS = 2 * B * L * DIM * 3 * H * D
 PIN = True
+GN = 11
 
 
 def tile_selfattention_pa_t_kernel(tc, x, pe, qkv_w, qkv_b, q_scale, k_scale, out_0, out_1, out_2):
@@ -223,7 +224,9 @@ def tile_selfattention_pa_t_kernel(tc, x, pe, qkv_w, qkv_b, q_scale, k_scale, ou
 
         def pair_add(r):
             sm = spool.tile([P, 4 * RT, D], F32, name="sm", tag="sm")
-            nc.vector.tensor_tensor(out=sm[:], in0=prods[r][:, :, 0, :], in1=prods[r][:, :, 1, :], op=ALU.add)
+            pr = prods[r]
+            nc.gpsimd.tensor_tensor(out=sm[:, 0:GN, :], in0=pr[:, 0:GN, 0, :], in1=pr[:, 0:GN, 1, :], op=ALU.add)
+            nc.vector.tensor_tensor(out=sm[:, GN:, :], in0=pr[:, GN:, 0, :], in1=pr[:, GN:, 1, :], op=ALU.add)
             sums[r] = sm
 
         def scale_out(r):

@@ -20,6 +20,7 @@ ROUNDS = B * TPB // RT
 NX = 6
 FLOPS = 2 * B * L * DIM * 3 * H * D
 PIN = True
+GN_LAST = 5
 GN = 11
 
 
@@ -49,7 +50,11 @@ def tile_selfattention_pa_t_kernel(tc, x, pe, qkv_w, qkv_b, q_scale, k_scale, ou
             b, j = divmod(r, TPB // RT)
             xt = xpool.tile([P, RT * DIM], BF16, name="xt", tag="xt")
             src = x[b].rearrange("(p t) k -> p (t k)", t=TPB)
-            nc.sync.dma_start(out=xt[:], in_=src[:, j * RT * DIM:(j + 1) * RT * DIM])
+            c0 = j * RT * DIM
+            cuts = 2 if r == 0 else 1
+            w = RT * DIM // cuts
+            for c in range(cuts):
+                nc.sync.dma_start(out=xt[:, c * w:(c + 1) * w], in_=src[:, c0 + c * w:c0 + (c + 1) * w])
             xts[r] = xt
 
         ident = const.tile([P, P], F32, name="ident", tag="ident")
@@ -85,7 +90,7 @@ def tile_selfattention_pa_t_kernel(tc, x, pe, qkv_w, qkv_b, q_scale, k_scale, ou
                     out=wg_qk[:, g].rearrange("p (n b i) t -> p n b i t", n=4, b=2)[:, :, b],
                     in_=w_raw[:, 4 * g:4 * g + 4, 0:256].rearrange("p t (n i b) -> p n i t b", i=32, b=2)[:, :, :, :, b],
                 )
-            nc.vector.tensor_copy(out=wg_v[:, g], in_=w_raw[:, 4 * g:4 * g + 4, 256:384].rearrange("p t n -> p n t"))
+            nc.scalar.copy(out=wg_v[:, g], in_=w_raw[:, 4 * g:4 * g + 4, 256:384].rearrange("p t n -> p n t"))
         wc_qk = const.tile([P, 512], U32, name="wc_qk", tag="wc_qk", align_bytes=64)
         ws_qk = const.tile([P, 512], U8, name="ws_qk", tag="ws_qk", align_bytes=64)
         wc_v = const.tile([P, 256], U32, name="wc_v", tag="wc_v", align_bytes=64)
@@ -104,9 +109,9 @@ def tile_selfattention_pa_t_kernel(tc, x, pe, qkv_w, qkv_b, q_scale, k_scale, ou
         nc.vector.tensor_copy(out=cv[:], in_=cps[:, 256:512])
 
         tab = const.tile([P, TPB, 2, 2, D], F32, name="tab", tag="tab")
-        for s in range(2):
+        def table(s, b):
             eng = nc.vector if s == 0 else nc.gpsimd
-            for b in range(2):
+            if True:
                 gain = cv[:, 128 + s * D:128 + (s + 1) * D].rearrange("p (i b) -> p b i", b=2)[:, b, :]
                 eng.tensor_tensor(
                     out=tab[:, :, s, b, :].rearrange("p t (a i) -> p t a i", a=2),
@@ -138,11 +143,17 @@ def tile_selfattention_pa_t_kernel(tc, x, pe, qkv_w, qkv_b, q_scale, k_scale, ou
                 )
             groupeds[r] = grouped
 
-        def quantise(r):
+        def quantise_tiles(r):
             xc = cpool.tile([P, RT * 256], U32, name="xc", tag="xc", align_bytes=64)
             xs = cpool.tile([P, RT * 256], U8, name="xs", tag="xs", align_bytes=64)
-            nc.vector.quantize_mx(out=xc[:].bitcast(FP8X4), scales=xs[:], in_=groupeds[r][:])
             codes[r], planes[r] = xc, xs
+
+        def quantise_part(r, c, cuts):
+            w = RT * 256 // cuts
+            nc.vector.quantize_mx(
+                out=codes[r][:, c * w:(c + 1) * w].bitcast(FP8X4), scales=planes[r][:, c * w:(c + 1) * w],
+                in_=groupeds[r][:, 4 * c * w:4 * (c + 1) * w],
+            )
 
         def project(r):
             xc, xs = codes[r], planes[r]
@@ -168,11 +179,27 @@ def tile_selfattention_pa_t_kernel(tc, x, pe, qkv_w, qkv_b, q_scale, k_scale, ou
                     )
             qkbanks[r], vbanks[r] = qk, vb
 
-        def store(dst, st, r):
-            b, j = divmod(r, TPB // RT)
-            hb = j // 2
+        def group_of(r):
+            return (r, 1) if r >= ROUNDS - 2 else (r - r % 2, 2)
+
+        def stage_tile(kind, r):
+            first, count = group_of(r)
+            if r == first:
+                st = stage.tile([P, H, 2 * RT, D], F32, name=kind, tag=kind)
+                stages[kind, first] = st
+            return stages[kind, first], (r - first) * RT
+
+        def store(dst, kind, r):
+            first, count = group_of(r)
+            if r != first + count - 1:
+                return
+            b, j = divmod(first, TPB // RT)
             view = dst[b].rearrange("h (p t) d -> p h (t d)", t=TPB)
-            nc.sync.dma_start(out=view[:, :, hb * 512:(hb + 1) * 512], in_=st[:].rearrange("p h t d -> p h (t d)"))
+            nt = count * RT
+            nc.sync.dma_start(
+                out=view[:, :, j * RT * D:(j * RT + nt) * D],
+                in_=stages[kind, first][:, :, 0:nt, :].rearrange("p h t d -> p h (t d)"),
+            )
 
         def add_bias(r):
             y = ypool.tile([P, RT, 256], F32, name="y", tag="y")
@@ -184,19 +211,14 @@ def tile_selfattention_pa_t_kernel(tc, x, pe, qkv_w, qkv_b, q_scale, k_scale, ou
                     op=ALU.add,
                 )
             ys[r] = y
-            if r % 2 == 0:
-                vst = stage.tile([P, H, 2 * RT, D], F32, name="vst", tag="vst")
-                stages["v", r // 2] = vst
-            vst = stages["v", r // 2]
-            tl = (r % 2) * RT
+            vst, tl = stage_tile("vst", r)
             nc.vector.tensor_tensor(
                 out=vst[:, :, tl:tl + RT, :].rearrange("p h t d -> p t h d"),
                 in0=vbanks[r][:].rearrange("p (t h d) -> p t h d", t=RT, h=H),
                 in1=cv[:, 0:128].rearrange("p (h d) -> p h d", h=H).unsqueeze(1).to_broadcast([P, RT, H, D]),
                 op=ALU.add,
             )
-            if r % 2 == 1:
-                store(out_2, vst, r)
+            store(out_2, "vst", r)
 
         def squares(r):
             ss = small.tile([P, 4 * RT], F32, name="ss", tag="ss")
@@ -225,38 +247,54 @@ def tile_selfattention_pa_t_kernel(tc, x, pe, qkv_w, qkv_b, q_scale, k_scale, ou
         def pair_add(r):
             sm = spool.tile([P, 4 * RT, D], F32, name="sm", tag="sm")
             pr = prods[r]
-            nc.gpsimd.tensor_tensor(out=sm[:, 0:GN, :], in0=pr[:, 0:GN, 0, :], in1=pr[:, 0:GN, 1, :], op=ALU.add)
-            nc.vector.tensor_tensor(out=sm[:, GN:, :], in0=pr[:, GN:, 0, :], in1=pr[:, GN:, 1, :], op=ALU.add)
+            gn = GN_LAST if r == ROUNDS - 1 else GN
+            nc.gpsimd.tensor_tensor(out=sm[:, 0:gn, :], in0=pr[:, 0:gn, 0, :], in1=pr[:, 0:gn, 1, :], op=ALU.add)
+            nc.vector.tensor_tensor(out=sm[:, gn:, :], in0=pr[:, gn:, 0, :], in1=pr[:, gn:, 1, :], op=ALU.add)
             sums[r] = sm
 
         def scale_out(r):
-            if r % 2 == 0:
-                qst = stage.tile([P, H, 2 * RT, D], F32, name="qst", tag="qst")
-                kst = stage.tile([P, H, 2 * RT, D], F32, name="kst", tag="kst")
-                stages["q", r // 2], stages["k", r // 2] = qst, kst
-            sts = (stages["q", r // 2], stages["k", r // 2])
-            tl = (r % 2) * RT
+            qst, tl = stage_tile("qst", r)
+            kst, tl = stage_tile("kst", r)
+            sts = (qst, kst)
             for n in range(4 * RT):
                 tt, s, h = n // 4, (n // 2) % 2, n % 2
-                nc.scalar.activation(
-                    out=sts[s][:, h, tl + tt, :].rearrange("p (i a) -> p i a", a=2),
-                    in_=sums[r][:, n, :].rearrange("p (a i) -> p i a", a=2),
-                    func=ACT.Copy, scale=rrs[r][:, n:n + 1],
-                )
-            if r % 2 == 1:
-                store(out_0, sts[0], r)
-                store(out_1, sts[1], r)
+                dst = sts[s][:, h, tl + tt, :].rearrange("p (i a) -> p i a", a=2)
+                src = sums[r][:, n, :].rearrange("p (a i) -> p i a", a=2)
+                if r == ROUNDS - 1 and s == 1:
+                    nc.vector.tensor_scalar(out=dst, in0=src, scalar1=rrs[r][:, n:n + 1], scalar2=None, op0=ALU.mult)
+                else:
+                    nc.scalar.activation(out=dst, in_=src, func=ACT.Copy, scale=rrs[r][:, n:n + 1])
+            store(out_0, "qst", r)
+            store(out_1, "kst", r)
 
         def live(r):
             return 0 <= r < ROUNDS
 
+        def quantise(r):
+            quantise_tiles(r)
+            quantise_part(r, 0, 1)
+
         transposes(0)
-        for i in range(-2, ROUNDS + 1):
+        copy_out(0)
+        table(1, 0)
+        table(1, 1)
+        quantise_tiles(0)
+        quantise_part(0, 0, 2)
+        table(0, 0)
+        quantise_part(0, 1, 2)
+        table(0, 1)
+        project(0)
+        transposes(1)
+        copy_out(1)
+        transposes(2)
+        for i in range(0, ROUNDS + 1):
             if live(i + 2):
                 copy_out(i + 2)
+            if i == 0:
+                add_bias(0)
             if live(i + 1):
                 quantise(i + 1)
-            if live(i):
+            if live(i) and i > 0:
                 add_bias(i)
             if live(i + 1):
                 project(i + 1)

@@ -287,7 +287,9 @@ def tile_selfattention_pa_t_kernel(tc, x, pe, qkv_w, qkv_b, q_scale, k_scale, ou
         transposes(1)
         copy_out(1)
         transposes(2)
-        for i in range(0, ROUNDS + 1):
+        for i in range(0, ROUNDS + 2):
+            if live(i - 2):
+                scale_out(i - 2)
             if live(i + 2):
                 copy_out(i + 2)
             if i == 0:
@@ -304,6 +306,5 @@ def tile_selfattention_pa_t_kernel(tc, x, pe, qkv_w, qkv_b, q_scale, k_scale, ou
                 squares(i)
             if live(i - 1):
                 pair_add(i - 1)
-                scale_out(i - 1)
             if live(i):
                 products(i)

@@ -16,12 +16,17 @@ EPS = 1e-6
 P = 128
 TPB = L // P
 RT = 4
-ROUNDS = B * TPB // RT
+RPB = TPB // RT
+ROUNDS = B * RPB
+GROUPS = RT * 2 * H
+QK = 2 * H * D
+PAIRS = D // 2
+WORDS = DIM // 2
+BANK = 512
 NX = 6
+GPSIMD_GROUPS = 11
+GPSIMD_GROUPS_LAST = 5
 FLOPS = 2 * B * L * DIM * 3 * H * D
-PIN = True
-GN_LAST = 5
-GN = 11
 
 
 def tile_selfattention_pa_t_kernel(tc, x, pe, qkv_w, qkv_b, q_scale, k_scale, out_0, out_1, out_2):
@@ -29,7 +34,7 @@ def tile_selfattention_pa_t_kernel(tc, x, pe, qkv_w, qkv_b, q_scale, k_scale, ou
     with ExitStack() as ctx:
         const = ctx.enter_context(tc.tile_pool(name="const", bufs=1))
         xpool = ctx.enter_context(tc.tile_pool(name="xpool", bufs=NX))
-        gpool = ctx.enter_context(tc.tile_pool(name="gpool", bufs=2))
+        gpool = ctx.enter_context(tc.tile_pool(name="gpool", bufs=3))
         cpool = ctx.enter_context(tc.tile_pool(name="cpool", bufs=2))
         ypool = ctx.enter_context(tc.tile_pool(name="ypool", bufs=2))
         ppool = ctx.enter_context(tc.tile_pool(name="ppool", bufs=2))
@@ -40,85 +45,87 @@ def tile_selfattention_pa_t_kernel(tc, x, pe, qkv_w, qkv_b, q_scale, k_scale, ou
         psum_tp = ctx.enter_context(tc.psum_pool(name="psum_tp", bufs=4))
         psum_qk = ctx.enter_context(tc.psum_pool(name="psum_qk", bufs=2))
         psum_v = ctx.enter_context(tc.psum_pool(name="psum_v", bufs=2))
-        if PIN:
-            ctx.enter_context(tc.manual_schedule())
+        ctx.enter_context(tc.manual_schedule())
 
         xts, tps, groupeds, codes, planes = {}, {}, {}, {}, {}
         qkbanks, vbanks, ys, prods, sums, rrs, stages = {}, {}, {}, {}, {}, {}, {}
 
         def load(r):
-            b, j = divmod(r, TPB // RT)
+            b, j = divmod(r, RPB)
             xt = xpool.tile([P, RT * DIM], BF16, name="xt", tag="xt")
             src = x[b].rearrange("(p t) k -> p (t k)", t=TPB)
-            c0 = j * RT * DIM
+            first = j * RT * DIM
             cuts = 2 if r == 0 else 1
-            w = RT * DIM // cuts
+            width = RT * DIM // cuts
             for c in range(cuts):
-                nc.sync.dma_start(out=xt[:, c * w:(c + 1) * w], in_=src[:, c0 + c * w:c0 + (c + 1) * w])
+                nc.sync.dma_start(
+                    out=xt[:, c * width:(c + 1) * width],
+                    in_=src[:, first + c * width:first + (c + 1) * width],
+                )
             xts[r] = xt
 
         ident = const.tile([P, P], F32, name="ident", tag="ident")
         make_identity(nc, ident[:])
         ones = const.tile([P, P], BF16, name="ones", tag="ones")
         nc.vector.memset(ones[:], 1.0)
-        row = const.tile([P, 512], BF16, name="row", tag="row")
+        row = const.tile([P, BANK], BF16, name="row", tag="row")
         nc.vector.memset(row[:], 0.0)
         eps = const.tile([P, 1], F32, name="eps", tag="eps")
         nc.vector.memset(eps[:], EPS)
         junk = const.tile([P, D], F32, name="junk", tag="junk")
 
-        w_raw = const.tile([P, 8, 384], BF16, name="w_raw", tag="w_raw")
+        w_raw = const.tile([P, 8, 3 * P], BF16, name="w_raw", tag="w_raw")
         nc.sync.dma_start(
             out=w_raw[:].rearrange("p (c e) n -> p c (e n)", e=2),
             in_=qkv_w.rearrange("(c q e) n -> q c (e n)", c=4, e=2),
         )
-        nc.sync.dma_start(out=row[0:1, 0:384], in_=qkv_b.unsqueeze(0))
-        nc.sync.dma_start(out=row[0:1, 384:448], in_=q_scale.unsqueeze(0))
-        nc.sync.dma_start(out=row[0:1, 448:512], in_=k_scale.unsqueeze(0))
+        nc.sync.dma_start(out=row[0:1, 0:3 * P], in_=qkv_b.unsqueeze(0))
+        nc.sync.dma_start(out=row[0:1, 3 * P:3 * P + D], in_=q_scale.unsqueeze(0))
+        nc.sync.dma_start(out=row[0:1, 3 * P + D:BANK], in_=k_scale.unsqueeze(0))
         load(0)
-        pe_sb = const.tile([P, TPB * 128], BF16, name="pe_sb", tag="pe_sb")
+        pe_sb = const.tile([P, TPB * 4 * PAIRS], BF16, name="pe_sb", tag="pe_sb")
         nc.sync.dma_start(out=pe_sb[:], in_=pe[0, 0].rearrange("(p t) i a b -> p (t i a b)", t=TPB))
         for r in range(1, NX):
             load(r)
         nc.scalar.activation(out=junk[:, 0:1], in_=eps[:], func=ACT.Abs_reciprocal_sqrt)
 
-        wg_qk = const.tile([P, 2, 256, 4], BF16, name="wg_qk", tag="wg_qk", align_bytes=64)
-        wg_v = const.tile([P, 2, 128, 4], BF16, name="wg_v", tag="wg_v", align_bytes=64)
+        wg_qk = const.tile([P, 2, QK, 4], BF16, name="wg_qk", tag="wg_qk", align_bytes=64)
+        wg_v = const.tile([P, 2, P, 4], BF16, name="wg_v", tag="wg_v", align_bytes=64)
         for g in range(2):
             for b in range(2):
                 nc.vector.tensor_copy(
                     out=wg_qk[:, g].rearrange("p (n b i) t -> p n b i t", n=4, b=2)[:, :, b],
-                    in_=w_raw[:, 4 * g:4 * g + 4, 0:256].rearrange("p t (n i b) -> p n i t b", i=32, b=2)[:, :, :, :, b],
+                    in_=w_raw[:, 4 * g:4 * g + 4, 0:QK].rearrange("p t (n i b) -> p n i t b", i=PAIRS, b=2)[:, :, :, :, b],
                 )
-            nc.scalar.copy(out=wg_v[:, g], in_=w_raw[:, 4 * g:4 * g + 4, 256:384].rearrange("p t n -> p n t"))
-        wc_qk = const.tile([P, 512], U32, name="wc_qk", tag="wc_qk", align_bytes=64)
-        ws_qk = const.tile([P, 512], U8, name="ws_qk", tag="ws_qk", align_bytes=64)
-        wc_v = const.tile([P, 256], U32, name="wc_v", tag="wc_v", align_bytes=64)
-        ws_v = const.tile([P, 256], U8, name="ws_v", tag="ws_v", align_bytes=64)
+            nc.scalar.copy(out=wg_v[:, g], in_=w_raw[:, 4 * g:4 * g + 4, QK:3 * P].rearrange("p t n -> p n t"))
+        wc_qk = const.tile([P, 2 * QK], U32, name="wc_qk", tag="wc_qk", align_bytes=64)
+        ws_qk = const.tile([P, 2 * QK], U8, name="ws_qk", tag="ws_qk", align_bytes=64)
+        wc_v = const.tile([P, 2 * P], U32, name="wc_v", tag="wc_v", align_bytes=64)
+        ws_v = const.tile([P, 2 * P], U8, name="ws_v", tag="ws_v", align_bytes=64)
         nc.vector.quantize_mx(out=wc_qk[:].bitcast(FP8X4), scales=ws_qk[:], in_=wg_qk[:].rearrange("p g n t -> p (g n t)"))
         nc.vector.quantize_mx(out=wc_v[:].bitcast(FP8X4), scales=ws_v[:], in_=wg_v[:].rearrange("p g n t -> p (g n t)"))
 
-        cps = psum_v.tile([P, 512], F32, name="cps", tag="vb")
+        cps = psum_v.tile([P, BANK], F32, name="cps", tag="vb")
         nc.tensor.matmul(out=cps[:], lhsT=ones[:], rhs=row[:], start=True, stop=True)
-        bias_qk = const.tile([P, 256], F32, name="bias_qk", tag="bias_qk")
+        bias_qk = const.tile([P, QK], F32, name="bias_qk", tag="bias_qk")
         nc.vector.tensor_copy(
-            out=bias_qk[:].rearrange("p (n b i) -> p n b i", b=2, i=32),
-            in_=cps[:, 0:256].rearrange("p (n i b) -> p n b i", i=32, b=2),
+            out=bias_qk[:].rearrange("p (n b i) -> p n b i", b=2, i=PAIRS),
+            in_=cps[:, 0:QK].rearrange("p (n i b) -> p n b i", i=PAIRS, b=2),
         )
-        cv = const.tile([P, 256], F32, name="cv", tag="cv")
-        nc.vector.tensor_copy(out=cv[:], in_=cps[:, 256:512])
+        cv = const.tile([P, QK], F32, name="cv", tag="cv")
+        nc.vector.tensor_copy(out=cv[:], in_=cps[:, QK:BANK])
 
         tab = const.tile([P, TPB, 2, 2, D], F32, name="tab", tag="tab")
+
         def table(s, b):
-            eng = nc.vector if s == 0 else nc.gpsimd
-            if True:
-                gain = cv[:, 128 + s * D:128 + (s + 1) * D].rearrange("p (i b) -> p b i", b=2)[:, b, :]
-                eng.tensor_tensor(
-                    out=tab[:, :, s, b, :].rearrange("p t (a i) -> p t a i", a=2),
-                    in0=pe_sb[:].rearrange("p (t i a b) -> p t a i b", i=32, a=2, b=2)[:, :, :, :, b],
-                    in1=gain.unsqueeze(1).unsqueeze(1).to_broadcast([P, TPB, 2, 32]),
-                    op=ALU.mult,
-                )
+            engine = nc.vector if s == 0 else nc.gpsimd
+            gain = cv[:, P + s * D:P + (s + 1) * D].rearrange("p (i b) -> p b i", b=2)[:, b, :]
+            engine.tensor_tensor(
+                out=tab[:, :, s, b, :].rearrange("p t (a i) -> p t a i", a=2),
+                in0=pe_sb[:].rearrange("p (t i a b) -> p t a i b", i=PAIRS, a=2, b=2)[:, :, :, :, b],
+                in1=gain.unsqueeze(1).unsqueeze(1).to_broadcast([P, TPB, 2, PAIRS]),
+                op=ALU.mult,
+            )
 
         def transposes(r):
             words = xts[r][:].bitcast(F32)
@@ -126,7 +133,7 @@ def tile_selfattention_pa_t_kernel(tc, x, pe, qkv_w, qkv_b, q_scale, k_scale, ou
             for tt in range(RT):
                 tp = psum_tp.tile([P, 4, P], F32, name="tp", tag="tp")
                 for c in range(4):
-                    col = tt * 512 + c * P
+                    col = tt * WORDS + c * P
                     nc.tensor.transpose(tp[:, c, :], words[:, col:col + P], ident[:])
                 banks.append(tp)
             tps[r] = banks
@@ -138,37 +145,40 @@ def tile_selfattention_pa_t_kernel(tc, x, pe, qkv_w, qkv_b, q_scale, k_scale, ou
             gw = grouped[:].bitcast(F32)
             for tt in range(RT):
                 nc.scalar.copy(
-                    out=gw[:, tt * 512:(tt + 1) * 512].rearrange("p (g r u) -> p g r u", g=2, u=2),
+                    out=gw[:, tt * WORDS:(tt + 1) * WORDS].rearrange("p (g r u) -> p g r u", g=2, u=2),
                     in_=tps[r][tt][:].rearrange("p (g u) r -> p g r u", u=2),
                 )
             groupeds[r] = grouped
 
-        def quantise_tiles(r):
-            xc = cpool.tile([P, RT * 256], U32, name="xc", tag="xc", align_bytes=64)
-            xs = cpool.tile([P, RT * 256], U8, name="xs", tag="xs", align_bytes=64)
+        def quantise(r, cuts):
+            xc = cpool.tile([P, RT * 2 * P], U32, name="xc", tag="xc", align_bytes=64)
+            xs = cpool.tile([P, RT * 2 * P], U8, name="xs", tag="xs", align_bytes=64)
             codes[r], planes[r] = xc, xs
+            width = RT * 2 * P // cuts
 
-        def quantise_part(r, c, cuts):
-            w = RT * 256 // cuts
-            nc.vector.quantize_mx(
-                out=codes[r][:, c * w:(c + 1) * w].bitcast(FP8X4), scales=planes[r][:, c * w:(c + 1) * w],
-                in_=groupeds[r][:, 4 * c * w:4 * (c + 1) * w],
-            )
+            def part(c):
+                nc.vector.quantize_mx(
+                    out=xc[:, c * width:(c + 1) * width].bitcast(FP8X4),
+                    scales=xs[:, c * width:(c + 1) * width],
+                    in_=groupeds[r][:, 4 * c * width:4 * (c + 1) * width],
+                )
+
+            return part
 
         def project(r):
             xc, xs = codes[r], planes[r]
             qk = []
-            for hf in range(2):
-                qkb = psum_qk.tile([P, 512], F32, name="qkb", tag="qkb")
+            for half in range(2):
+                qkb = psum_qk.tile([P, BANK], F32, name="qkb", tag="qkb")
                 qk.append(qkb)
-            vb = psum_v.tile([P, 512], F32, name="vb", tag="vb")
+            vb = psum_v.tile([P, BANK], F32, name="vb", tag="vb")
             for tt in range(RT):
                 for g in range(2):
                     sl = slice((tt * 2 + g) * P, (tt * 2 + g + 1) * P)
                     nc.tensor.matmul_mx(
-                        out=qk[tt // 2][:, (tt % 2) * 256:(tt % 2 + 1) * 256],
+                        out=qk[tt // 2][:, (tt % 2) * QK:(tt % 2 + 1) * QK],
                         lhsT=xc[:, sl].bitcast(FP8X4), lhsT_scale=xs[:, sl],
-                        rhs=wc_qk[:, g * 256:(g + 1) * 256].bitcast(FP8X4), rhs_scale=ws_qk[:, g * 256:(g + 1) * 256],
+                        rhs=wc_qk[:, g * QK:(g + 1) * QK].bitcast(FP8X4), rhs_scale=ws_qk[:, g * QK:(g + 1) * QK],
                         start=(g == 0), stop=(g == 1),
                     )
                     nc.tensor.matmul_mx(
@@ -179,21 +189,21 @@ def tile_selfattention_pa_t_kernel(tc, x, pe, qkv_w, qkv_b, q_scale, k_scale, ou
                     )
             qkbanks[r], vbanks[r] = qk, vb
 
-        def group_of(r):
+        def stored_with(r):
             return (r, 1) if r >= ROUNDS - 2 else (r - r % 2, 2)
 
         def stage_tile(kind, r):
-            first, count = group_of(r)
+            first, count = stored_with(r)
             if r == first:
                 st = stage.tile([P, H, 2 * RT, D], F32, name=kind, tag=kind)
                 stages[kind, first] = st
             return stages[kind, first], (r - first) * RT
 
         def store(dst, kind, r):
-            first, count = group_of(r)
+            first, count = stored_with(r)
             if r != first + count - 1:
                 return
-            b, j = divmod(first, TPB // RT)
+            b, j = divmod(first, RPB)
             view = dst[b].rearrange("h (p t) d -> p h (t d)", t=TPB)
             nt = count * RT
             nc.sync.dma_start(
@@ -202,12 +212,12 @@ def tile_selfattention_pa_t_kernel(tc, x, pe, qkv_w, qkv_b, q_scale, k_scale, ou
             )
 
         def add_bias(r):
-            y = ypool.tile([P, RT, 256], F32, name="y", tag="y")
-            for hf in range(2):
+            y = ypool.tile([P, RT, QK], F32, name="y", tag="y")
+            for half in range(2):
                 nc.vector.tensor_tensor(
-                    out=y[:, 2 * hf:2 * hf + 2, :],
-                    in0=qkbanks[r][hf][:].rearrange("p (t c) -> p t c", t=2),
-                    in1=bias_qk[:].unsqueeze(1).to_broadcast([P, 2, 256]),
+                    out=y[:, 2 * half:2 * half + 2, :],
+                    in0=qkbanks[r][half][:].rearrange("p (t c) -> p t c", t=2),
+                    in1=bias_qk[:].unsqueeze(1).to_broadcast([P, 2, QK]),
                     op=ALU.add,
                 )
             ys[r] = y
@@ -215,27 +225,27 @@ def tile_selfattention_pa_t_kernel(tc, x, pe, qkv_w, qkv_b, q_scale, k_scale, ou
             nc.vector.tensor_tensor(
                 out=vst[:, :, tl:tl + RT, :].rearrange("p h t d -> p t h d"),
                 in0=vbanks[r][:].rearrange("p (t h d) -> p t h d", t=RT, h=H),
-                in1=cv[:, 0:128].rearrange("p (h d) -> p h d", h=H).unsqueeze(1).to_broadcast([P, RT, H, D]),
+                in1=cv[:, 0:P].rearrange("p (h d) -> p h d", h=H).unsqueeze(1).to_broadcast([P, RT, H, D]),
                 op=ALU.add,
             )
             store(out_2, "vst", r)
 
         def squares(r):
-            ss = small.tile([P, 4 * RT], F32, name="ss", tag="ss")
-            sq = jpool.tile([P, 4 * RT, D], F32, name="sq", tag="sq")
-            for n in range(4 * RT):
+            ss = small.tile([P, GROUPS], F32, name="ss", tag="ss")
+            sq = jpool.tile([P, GROUPS, D], F32, name="sq", tag="sq")
+            for n in range(GROUPS):
                 nc.scalar.activation(
                     out=sq[:, n, :], in_=ys[r][:, n // 4, (n % 4) * D:(n % 4 + 1) * D],
                     func=ACT.Square, accum_out=ss[:, n:n + 1],
                 )
-            rr = small.tile([P, 4 * RT], F32, name="rr", tag="rr")
+            rr = small.tile([P, GROUPS], F32, name="rr", tag="rr")
             nc.scalar.activation(out=rr[:], in_=ss[:], func=ACT.Abs_reciprocal_sqrt, scale=1.0 / D, bias=eps[:])
             rrs[r] = rr
 
         def products(r):
-            t0 = (r % (TPB // RT)) * RT
-            pr = ppool.tile([P, 4 * RT, 2, D], F32, name="pr", tag="pr")
-            shape = [P, 2 * RT, H, 2, 2, 32]
+            t0 = (r % RPB) * RT
+            pr = ppool.tile([P, GROUPS, 2, D], F32, name="pr", tag="pr")
+            shape = [P, 2 * RT, H, 2, 2, PAIRS]
             nc.vector.tensor_tensor(
                 out=pr[:].rearrange("p (m h) b (a i) -> p m h b a i", h=H, a=2),
                 in0=ys[r][:].rearrange("p t (s h b i) -> p (t s) h b i", s=2, h=H, b=2).unsqueeze(4).to_broadcast(shape),
@@ -245,9 +255,9 @@ def tile_selfattention_pa_t_kernel(tc, x, pe, qkv_w, qkv_b, q_scale, k_scale, ou
             prods[r] = pr
 
         def pair_add(r):
-            sm = spool.tile([P, 4 * RT, D], F32, name="sm", tag="sm")
+            sm = spool.tile([P, GROUPS, D], F32, name="sm", tag="sm")
             pr = prods[r]
-            gn = GN_LAST if r == ROUNDS - 1 else GN
+            gn = GPSIMD_GROUPS_LAST if r == ROUNDS - 1 else GPSIMD_GROUPS
             nc.gpsimd.tensor_tensor(out=sm[:, 0:gn, :], in0=pr[:, 0:gn, 0, :], in1=pr[:, 0:gn, 1, :], op=ALU.add)
             nc.vector.tensor_tensor(out=sm[:, gn:, :], in0=pr[:, gn:, 0, :], in1=pr[:, gn:, 1, :], op=ALU.add)
             sums[r] = sm
@@ -256,7 +266,7 @@ def tile_selfattention_pa_t_kernel(tc, x, pe, qkv_w, qkv_b, q_scale, k_scale, ou
             qst, tl = stage_tile("qst", r)
             kst, tl = stage_tile("kst", r)
             sts = (qst, kst)
-            for n in range(4 * RT):
+            for n in range(GROUPS):
                 tt, s, h = n // 4, (n // 2) % 2, n % 2
                 dst = sts[s][:, h, tl + tt, :].rearrange("p (i a) -> p i a", a=2)
                 src = sums[r][:, n, :].rearrange("p (a i) -> p i a", a=2)
@@ -270,41 +280,38 @@ def tile_selfattention_pa_t_kernel(tc, x, pe, qkv_w, qkv_b, q_scale, k_scale, ou
         def live(r):
             return 0 <= r < ROUNDS
 
-        def quantise(r):
-            quantise_tiles(r)
-            quantise_part(r, 0, 1)
-
         transposes(0)
         copy_out(0)
         table(1, 0)
         table(1, 1)
-        quantise_tiles(0)
-        quantise_part(0, 0, 2)
+        part = quantise(0, 2)
+        part(0)
         table(0, 0)
-        quantise_part(0, 1, 2)
+        part(1)
         table(0, 1)
-        project(0)
         transposes(1)
+        project(0)
         copy_out(1)
         transposes(2)
-        for i in range(0, ROUNDS + 2):
-            if live(i - 2):
-                scale_out(i - 2)
-            if live(i + 2):
-                copy_out(i + 2)
+        copy_out(2)
+        transposes(3)
+        for i in range(0, ROUNDS + 1):
+            if live(i + 3):
+                copy_out(i + 3)
             if i == 0:
                 add_bias(0)
             if live(i + 1):
-                quantise(i + 1)
+                quantise(i + 1, 1)(0)
             if live(i) and i > 0:
                 add_bias(i)
             if live(i + 1):
                 project(i + 1)
-            if live(i + 3):
-                transposes(i + 3)
+            if live(i + 4):
+                transposes(i + 4)
             if live(i):
                 squares(i)
             if live(i - 1):
                 pair_add(i - 1)
+                scale_out(i - 1)
             if live(i):
                 products(i)

@@ -118,9 +118,8 @@ def tile_selfattention_pa_t_kernel(tc, x, pe, qkv_w, qkv_b, q_scale, k_scale, ou
         tab = const.tile([P, TPB, 2, 2, D], F32, name="tab", tag="tab")
 
         def table(s, b):
-            engine = nc.vector if s == 0 else nc.gpsimd
             gain = cv[:, P + s * D:P + (s + 1) * D].rearrange("p (i b) -> p b i", b=2)[:, b, :]
-            engine.tensor_tensor(
+            nc.vector.tensor_tensor(
                 out=tab[:, :, s, b, :].rearrange("p t (a i) -> p t a i", a=2),
                 in0=pe_sb[:].rearrange("p (t i a b) -> p t a i b", i=PAIRS, a=2, b=2)[:, :, :, :, b],
                 in1=gain.unsqueeze(1).unsqueeze(1).to_broadcast([P, TPB, 2, PAIRS]),
@@ -282,13 +281,13 @@ def tile_selfattention_pa_t_kernel(tc, x, pe, qkv_w, qkv_b, q_scale, k_scale, ou
 
         transposes(0)
         copy_out(0)
-        table(1, 0)
-        table(1, 1)
         part = quantise(0, 2)
         part(0)
         table(0, 0)
         part(1)
         table(0, 1)
+        table(1, 0)
+        table(1, 1)
         transposes(1)
         project(0)
         copy_out(1)

from contextlib import ExitStack

import concourse.mybir as mybir
from concourse.masks import make_identity

F32 = mybir.dt.float32
BF16 = mybir.dt.bfloat16
U32 = mybir.dt.uint32
U8 = mybir.dt.uint8
FP8X4 = mybir.dt.float8_e4m3fn_x4
ALU = mybir.AluOpType
ACT = mybir.ActivationFunctionType

B, L, DIM, H, D = 4, 2048, 1024, 2, 64
EPS = 1e-6
P = 128
TPB = L // P
RT = 4
RPB = TPB // RT
ROUNDS = B * RPB
GROUPS = RT * 2 * H
QK = 2 * H * D
PAIRS = D // 2
WORDS = DIM // 2
BANK = 512
NX = 6
GPSIMD_GROUPS = 11
GPSIMD_GROUPS_LAST = 5
FLOPS = 2 * B * L * DIM * 3 * H * D


def tile_selfattention_pa_t_kernel(tc, x, pe, qkv_w, qkv_b, q_scale, k_scale, out_0, out_1, out_2):
    nc = tc.nc
    with ExitStack() as ctx:
        const = ctx.enter_context(tc.tile_pool(name="const", bufs=1))
        xpool = ctx.enter_context(tc.tile_pool(name="xpool", bufs=NX))
        gpool = ctx.enter_context(tc.tile_pool(name="gpool", bufs=3))
        cpool = ctx.enter_context(tc.tile_pool(name="cpool", bufs=2))
        ypool = ctx.enter_context(tc.tile_pool(name="ypool", bufs=2))
        ppool = ctx.enter_context(tc.tile_pool(name="ppool", bufs=2))
        spool = ctx.enter_context(tc.tile_pool(name="spool", bufs=2))
        jpool = ctx.enter_context(tc.tile_pool(name="jpool", bufs=2))
        small = ctx.enter_context(tc.tile_pool(name="small", bufs=3))
        stage = ctx.enter_context(tc.tile_pool(name="stage", bufs=2))
        psum_tp = ctx.enter_context(tc.psum_pool(name="psum_tp", bufs=4))
        psum_qk = ctx.enter_context(tc.psum_pool(name="psum_qk", bufs=2))
        psum_v = ctx.enter_context(tc.psum_pool(name="psum_v", bufs=2))
        ctx.enter_context(tc.manual_schedule())

        xts, tps, groupeds, codes, planes = {}, {}, {}, {}, {}
        qkbanks, vbanks, ys, prods, sums, rrs, stages = {}, {}, {}, {}, {}, {}, {}

        def load(r):
            b, j = divmod(r, RPB)
            xt = xpool.tile([P, RT * DIM], BF16, name="xt", tag="xt")
            src = x[b].rearrange("(p t) k -> p (t k)", t=TPB)
            first = j * RT * DIM
            cuts = 2 if r == 0 else 1
            width = RT * DIM // cuts
            for c in range(cuts):
                nc.sync.dma_start(
                    out=xt[:, c * width:(c + 1) * width],
                    in_=src[:, first + c * width:first + (c + 1) * width],
                )
            xts[r] = xt

        ident = const.tile([P, P], F32, name="ident", tag="ident")
        make_identity(nc, ident[:])
        ones = const.tile([P, P], BF16, name="ones", tag="ones")
        nc.vector.memset(ones[:], 1.0)
        row = const.tile([P, BANK], BF16, name="row", tag="row")
        nc.vector.memset(row[:], 0.0)
        eps = const.tile([P, 1], F32, name="eps", tag="eps")
        nc.vector.memset(eps[:], EPS)
        junk = const.tile([P, D], F32, name="junk", tag="junk")

        w_raw = const.tile([P, 8, 3 * P], BF16, name="w_raw", tag="w_raw")
        nc.sync.dma_start(
            out=w_raw[:].rearrange("p (c e) n -> p c (e n)", e=2),
            in_=qkv_w.rearrange("(c q e) n -> q c (e n)", c=4, e=2),
        )
        nc.sync.dma_start(out=row[0:1, 0:3 * P], in_=qkv_b.unsqueeze(0))
        nc.sync.dma_start(out=row[0:1, 3 * P:3 * P + D], in_=q_scale.unsqueeze(0))
        nc.sync.dma_start(out=row[0:1, 3 * P + D:BANK], in_=k_scale.unsqueeze(0))
        load(0)
        pe_sb = const.tile([P, TPB * 4 * PAIRS], BF16, name="pe_sb", tag="pe_sb")
        nc.sync.dma_start(out=pe_sb[:], in_=pe[0, 0].rearrange("(p t) i a b -> p (t i a b)", t=TPB))
        for r in range(1, NX):
            load(r)
        nc.scalar.activation(out=junk[:, 0:1], in_=eps[:], func=ACT.Abs_reciprocal_sqrt)

        wg_qk = const.tile([P, 2, QK, 4], BF16, name="wg_qk", tag="wg_qk", align_bytes=64)
        wg_v = const.tile([P, 2, P, 4], BF16, name="wg_v", tag="wg_v", align_bytes=64)
        for g in range(2):
            for b in range(2):
                nc.vector.tensor_copy(
                    out=wg_qk[:, g].rearrange("p (n b i) t -> p n b i t", n=4, b=2)[:, :, b],
                    in_=w_raw[:, 4 * g:4 * g + 4, 0:QK].rearrange("p t (n i b) -> p n i t b", i=PAIRS, b=2)[:, :, :, :, b],
                )
            nc.scalar.copy(out=wg_v[:, g], in_=w_raw[:, 4 * g:4 * g + 4, QK:3 * P].rearrange("p t n -> p n t"))
        wc_qk = const.tile([P, 2 * QK], U32, name="wc_qk", tag="wc_qk", align_bytes=64)
        ws_qk = const.tile([P, 2 * QK], U8, name="ws_qk", tag="ws_qk", align_bytes=64)
        wc_v = const.tile([P, 2 * P], U32, name="wc_v", tag="wc_v", align_bytes=64)
        ws_v = const.tile([P, 2 * P], U8, name="ws_v", tag="ws_v", align_bytes=64)
        nc.vector.quantize_mx(out=wc_qk[:].bitcast(FP8X4), scales=ws_qk[:], in_=wg_qk[:].rearrange("p g n t -> p (g n t)"))
        nc.vector.quantize_mx(out=wc_v[:].bitcast(FP8X4), scales=ws_v[:], in_=wg_v[:].rearrange("p g n t -> p (g n t)"))

        cps = psum_v.tile([P, BANK], F32, name="cps", tag="vb")
        nc.tensor.matmul(out=cps[:], lhsT=ones[:], rhs=row[:], start=True, stop=True)
        bias_qk = const.tile([P, QK], F32, name="bias_qk", tag="bias_qk")
        nc.vector.tensor_copy(
            out=bias_qk[:].rearrange("p (n b i) -> p n b i", b=2, i=PAIRS),
            in_=cps[:, 0:QK].rearrange("p (n i b) -> p n b i", i=PAIRS, b=2),
        )
        cv = const.tile([P, QK], F32, name="cv", tag="cv")
        nc.vector.tensor_copy(out=cv[:], in_=cps[:, QK:BANK])

        tab = const.tile([P, TPB, 2, 2, D], F32, name="tab", tag="tab")

        def table(s, b):
            gain = cv[:, P + s * D:P + (s + 1) * D].rearrange("p (i b) -> p b i", b=2)[:, b, :]
            nc.vector.tensor_tensor(
                out=tab[:, :, s, b, :].rearrange("p t (a i) -> p t a i", a=2),
                in0=pe_sb[:].rearrange("p (t i a b) -> p t a i b", i=PAIRS, a=2, b=2)[:, :, :, :, b],
                in1=gain.unsqueeze(1).unsqueeze(1).to_broadcast([P, TPB, 2, PAIRS]),
                op=ALU.mult,
            )

        def transposes(r):
            words = xts[r][:].bitcast(F32)
            banks = []
            for tt in range(RT):
                tp = psum_tp.tile([P, 4, P], F32, name="tp", tag="tp")
                for c in range(4):
                    col = tt * WORDS + c * P
                    nc.tensor.transpose(tp[:, c, :], words[:, col:col + P], ident[:])
                banks.append(tp)
            tps[r] = banks
            if r + NX < ROUNDS:
                load(r + NX)

        def copy_out(r):
            grouped = gpool.tile([P, RT * DIM], BF16, name="grouped", tag="grouped", align_bytes=64)
            gw = grouped[:].bitcast(F32)
            for tt in range(RT):
                nc.scalar.copy(
                    out=gw[:, tt * WORDS:(tt + 1) * WORDS].rearrange("p (g r u) -> p g r u", g=2, u=2),
                    in_=tps[r][tt][:].rearrange("p (g u) r -> p g r u", u=2),
                )
            groupeds[r] = grouped

        def quantise(r, cuts):
            xc = cpool.tile([P, RT * 2 * P], U32, name="xc", tag="xc", align_bytes=64)
            xs = cpool.tile([P, RT * 2 * P], U8, name="xs", tag="xs", align_bytes=64)
            codes[r], planes[r] = xc, xs
            width = RT * 2 * P // cuts

            def part(c):
                nc.vector.quantize_mx(
                    out=xc[:, c * width:(c + 1) * width].bitcast(FP8X4),
                    scales=xs[:, c * width:(c + 1) * width],
                    in_=groupeds[r][:, 4 * c * width:4 * (c + 1) * width],
                )

            return part

        def project(r):
            xc, xs = codes[r], planes[r]
            qk = []
            for half in range(2):
                qkb = psum_qk.tile([P, BANK], F32, name="qkb", tag="qkb")
                qk.append(qkb)
            vb = psum_v.tile([P, BANK], F32, name="vb", tag="vb")
            for tt in range(RT):
                for g in range(2):
                    sl = slice((tt * 2 + g) * P, (tt * 2 + g + 1) * P)
                    nc.tensor.matmul_mx(
                        out=qk[tt // 2][:, (tt % 2) * QK:(tt % 2 + 1) * QK],
                        lhsT=xc[:, sl].bitcast(FP8X4), lhsT_scale=xs[:, sl],
                        rhs=wc_qk[:, g * QK:(g + 1) * QK].bitcast(FP8X4), rhs_scale=ws_qk[:, g * QK:(g + 1) * QK],
                        start=(g == 0), stop=(g == 1),
                    )
                    nc.tensor.matmul_mx(
                        out=vb[:, tt * P:(tt + 1) * P],
                        lhsT=xc[:, sl].bitcast(FP8X4), lhsT_scale=xs[:, sl],
                        rhs=wc_v[:, g * P:(g + 1) * P].bitcast(FP8X4), rhs_scale=ws_v[:, g * P:(g + 1) * P],
                        start=(g == 0), stop=(g == 1),
                    )
            qkbanks[r], vbanks[r] = qk, vb

        def stored_with(r):
            return (r, 1) if r >= ROUNDS - 2 else (r - r % 2, 2)

        def stage_tile(kind, r):
            first, count = stored_with(r)
            if r == first:
                st = stage.tile([P, H, 2 * RT, D], F32, name=kind, tag=kind)
                stages[kind, first] = st
            return stages[kind, first], (r - first) * RT

        def store(dst, kind, r):
            first, count = stored_with(r)
            if r != first + count - 1:
                return
            b, j = divmod(first, RPB)
            view = dst[b].rearrange("h (p t) d -> p h (t d)", t=TPB)
            nt = count * RT
            nc.sync.dma_start(
                out=view[:, :, j * RT * D:(j * RT + nt) * D],
                in_=stages[kind, first][:, :, 0:nt, :].rearrange("p h t d -> p h (t d)"),
            )

        def add_bias(r):
            y = ypool.tile([P, RT, QK], F32, name="y", tag="y")
            for half in range(2):
                nc.vector.tensor_tensor(
                    out=y[:, 2 * half:2 * half + 2, :],
                    in0=qkbanks[r][half][:].rearrange("p (t c) -> p t c", t=2),
                    in1=bias_qk[:].unsqueeze(1).to_broadcast([P, 2, QK]),
                    op=ALU.add,
                )
            ys[r] = y
            vst, tl = stage_tile("vst", r)
            nc.vector.tensor_tensor(
                out=vst[:, :, tl:tl + RT, :].rearrange("p h t d -> p t h d"),
                in0=vbanks[r][:].rearrange("p (t h d) -> p t h d", t=RT, h=H),
                in1=cv[:, 0:P].rearrange("p (h d) -> p h d", h=H).unsqueeze(1).to_broadcast([P, RT, H, D]),
                op=ALU.add,
            )
            store(out_2, "vst", r)

        def squares(r):
            ss = small.tile([P, GROUPS], F32, name="ss", tag="ss")
            sq = jpool.tile([P, GROUPS, D], F32, name="sq", tag="sq")
            for n in range(GROUPS):
                nc.scalar.activation(
                    out=sq[:, n, :], in_=ys[r][:, n // 4, (n % 4) * D:(n % 4 + 1) * D],
                    func=ACT.Square, accum_out=ss[:, n:n + 1],
                )
            rr = small.tile([P, GROUPS], F32, name="rr", tag="rr")
            nc.scalar.activation(out=rr[:], in_=ss[:], func=ACT.Abs_reciprocal_sqrt, scale=1.0 / D, bias=eps[:])
            rrs[r] = rr

        def products(r):
            t0 = (r % RPB) * RT
            pr = ppool.tile([P, GROUPS, 2, D], F32, name="pr", tag="pr")
            shape = [P, 2 * RT, H, 2, 2, PAIRS]
            nc.vector.tensor_tensor(
                out=pr[:].rearrange("p (m h) b (a i) -> p m h b a i", h=H, a=2),
                in0=ys[r][:].rearrange("p t (s h b i) -> p (t s) h b i", s=2, h=H, b=2).unsqueeze(4).to_broadcast(shape),
                in1=tab[:, t0:t0 + RT].rearrange("p t s b (a i) -> p (t s) b a i", a=2).unsqueeze(2).to_broadcast(shape),
                op=ALU.mult,
            )
            prods[r] = pr

        def pair_add(r):
            sm = spool.tile([P, GROUPS, D], F32, name="sm", tag="sm")
            pr = prods[r]
            gn = GPSIMD_GROUPS_LAST if r == ROUNDS - 1 else GPSIMD_GROUPS
            nc.gpsimd.tensor_tensor(out=sm[:, 0:gn, :], in0=pr[:, 0:gn, 0, :], in1=pr[:, 0:gn, 1, :], op=ALU.add)
            nc.vector.tensor_tensor(out=sm[:, gn:, :], in0=pr[:, gn:, 0, :], in1=pr[:, gn:, 1, :], op=ALU.add)
            sums[r] = sm

        def scale_out(r):
            qst, tl = stage_tile("qst", r)
            kst, tl = stage_tile("kst", r)
            sts = (qst, kst)
            for n in range(GROUPS):
                tt, s, h = n // 4, (n // 2) % 2, n % 2
                dst = sts[s][:, h, tl + tt, :].rearrange("p (i a) -> p i a", a=2)
                src = sums[r][:, n, :].rearrange("p (a i) -> p i a", a=2)
                if r == ROUNDS - 1 and s == 1:
                    nc.vector.tensor_scalar(out=dst, in0=src, scalar1=rrs[r][:, n:n + 1], scalar2=None, op0=ALU.mult)
                else:
                    nc.scalar.activation(out=dst, in_=src, func=ACT.Copy, scale=rrs[r][:, n:n + 1])
            store(out_0, "qst", r)
            store(out_1, "kst", r)

        def live(r):
            return 0 <= r < ROUNDS

        transposes(0)
        copy_out(0)
        part = quantise(0, 2)
        part(0)
        table(0, 0)
        part(1)
        table(0, 1)
        table(1, 0)
        table(1, 1)
        transposes(1)
        project(0)
        copy_out(1)
        transposes(2)
        copy_out(2)
        transposes(3)
        for i in range(0, ROUNDS + 1):
            if live(i + 3):
                copy_out(i + 3)
            if i == 0:
                add_bias(0)
            if live(i + 1):
                quantise(i + 1, 1)(0)
            if live(i) and i > 0:
                add_bias(i)
            if live(i + 1):
                project(i + 1)
            if live(i + 4):
                transposes(i + 4)
            if live(i):
                squares(i)
            if live(i - 1):
                pair_add(i - 1)
                scale_out(i - 1)
            if live(i):
                products(i)
